import numpy as np
import ml_dtypes


def mxq(x, axis, fmt="e4m3"):
    dtype, down = {"e4m3": (ml_dtypes.float8_e4m3fn, 7), "e5m2": (ml_dtypes.float8_e5m2, 14)}[fmt]
    v = np.moveaxis(np.asarray(x, np.float32).astype(ml_dtypes.bfloat16).astype(np.float64), axis, -1)
    blocks = v.reshape(v.shape[:-1] + (-1, 32))
    amax = np.abs(blocks).max(-1, keepdims=True)
    byte = np.maximum(np.where(amax > 0, np.frexp(amax)[1] - 1 + 127, 0) - down, 1)
    scale = np.exp2(byte - 127.0)
    codes = (blocks / scale).astype(np.float32).astype(dtype).astype(np.float64)
    return np.moveaxis((codes * scale).reshape(v.shape), -1, axis)


WIDE = False


def mx_kscale(k):
    if not WIDE:
        return np.ones(k)
    levels = np.array([10, -10, 5, -5, 0])
    if k % 512:
        return np.exp2(np.random.permutation(np.resize(levels, k // 32))).repeat(32)
    a = np.empty((k // 512, 16))
    for p in range(k // 512):
        a[p, :8] = np.random.permutation(np.resize(levels, 8))
        for g in range(8):
            far = levels[np.abs(levels - a[p, g]) >= 10]
            a[p, g + 8] = far[np.random.randint(len(far))]
    return np.exp2(a.ravel()).repeat(32)


BF16 = ml_dtypes.bfloat16


def bf(x):
    return np.asarray(x, np.float32).astype(BF16)


def f64(x):
    return np.asarray(x).astype(np.float64)


T, K, E, H, KVH, D = 512, 1024, 2048, 16, 4, 128
EPS = 1e-05


def rmsnorm(x, w):
    var = np.mean(np.square(x), axis=-1, keepdims=True)
    return x * (1.0 / np.sqrt(var + EPS)) * w


def draw0():
    s = mx_kscale(E)
    return {"hidden_states": bf(np.random.standard_normal((T, E)) * s),
            "Wq": bf(np.random.standard_normal((H * D, E)) / np.sqrt(E) / s),
            "q_norm_w": bf(1.5 + 0.1 * np.random.standard_normal(D))}


def core(hidden_states, Wq, q_norm_w):
    q = mxq(f64(hidden_states), 1, "e4m3") @ mxq(f64(Wq), 1, "e4m3").T
    qh = rmsnorm(q.reshape(T, H, D), f64(q_norm_w))
    return qh.transpose(1, 0, 2)


def e4m3fn_bytes(y):
    return np.clip(np.asarray(y, np.float64), -448.0, 448.0).astype(np.float32).astype(ml_dtypes.float8_e4m3fn).view(np.uint8)


def e4m3fn_values(b):
    return np.asarray(b, np.uint8).view(ml_dtypes.float8_e4m3fn).astype(np.float64)


def setup_inputs():
    d = draw0()
    x0 = np.asarray(d['Wq']).astype(np.float64)
    s = (np.max(np.abs(x0), axis=(0,), keepdims=True) / 448.0).astype(np.float32)
    out = {}
    for k, v in d.items():
        if k == 'Wq':
            out['Wq_bytes'] = e4m3fn_bytes(x0 / s.astype(np.float64))
            out['Wq_scale'] = s
        else:
            out[k] = v
    return out


def reference(hidden_states, Wq_bytes, Wq_scale, q_norm_w):
    return core(hidden_states, e4m3fn_values(Wq_bytes) * Wq_scale.astype(np.float64), q_norm_w)

@@ -1,0 +1,263 @@
+from contextlib import ExitStack
+
+import concourse.mybir as mybir
+from concourse.masks import make_identity
+
+T, E, H, D = 512, 2048, 16, 128
+EPS = 1e-05
+FLOPS = 2 * T * E * H * D
+
+F32 = mybir.dt.float32
+BF16 = mybir.dt.bfloat16
+U32 = mybir.dt.uint32
+U8 = mybir.dt.uint8
+FP8 = mybir.dt.float8_e4m3fn
+FP8X4 = mybir.dt.float8_e4m3fn_x4
+ACT = mybir.ActivationFunctionType
+MULT = mybir.AluOpType.mult
+
+P = 128
+PACK = 4
+PASSES = E // (P * PACK)
+TOKEN_TILES = T // P
+CHUNK = 512
+
+SCALAR_TILES = (4, 10)
+
+TURN_LAG = 1
+QUANTIZE_LAG = 2
+MULTIPLY_LAG = 4
+FINISH_LAG = 5
+CAST_LEAD = 3
+SCALE_LEAD = 2
+INTERLEAVE_LEAD = 1
+TOKENS_TURNED = {1: (0, 1), 2: (2, 3)}
+TOKENS_QUANTIZED = {2: (0, 1), 3: (2, 3)}
+
+
+def tile_combcrossattention_pa_kernel(tc, hidden_states, Wq_bytes, Wq_scale, q_norm_w, out):
+    nc = tc.nc
+    with ExitStack() as ctx:
+        const = ctx.enter_context(tc.tile_pool(name="const", bufs=1))
+        keep = ctx.enter_context(tc.tile_pool(name="keep", bufs=1))
+        wide_pool = ctx.enter_context(tc.tile_pool(name="wide", bufs=5))
+        grouped_pool = ctx.enter_context(tc.tile_pool(name="grouped", bufs=5))
+        plane_pool = ctx.enter_context(tc.tile_pool(name="planes", bufs=2))
+        stat_pool = ctx.enter_context(tc.tile_pool(name="stat", bufs=6))
+        result_pool = ctx.enter_context(tc.tile_pool(name="result", bufs=4))
+        turn_psum = ctx.enter_context(tc.psum_pool(name="turn_psum", bufs=4))
+        acc_psum = ctx.enter_context(tc.psum_pool(name="acc_psum", bufs=4))
+
+        ident = const.tile([P, P], F32, name="ident")
+        make_identity(nc, ident[:])
+
+        one = const.tile([P, 1], F32, name="one")
+        nc.gpsimd.memset(one[:], 1.0)
+        warm = const.tile([P, 1], F32, name="warm")
+        nc.scalar.activation(out=warm[:], in_=one[:], func=ACT.Abs_reciprocal_sqrt)
+
+        scale_row = Wq_scale.rearrange("o k -> (o k)")
+        scale_all = const.tile([P, E], F32, name="scale_all")
+
+        gain_bf = const.tile([P, D], BF16, name="gain_bf")
+        nc.scalar.dma_start(out=gain_bf[:], in_=q_norm_w.partition_broadcast(P))
+
+        scale_cols = const.tile([P, PACK * PASSES], F32, name="scale_cols")
+        nc.scalar.dma_start(
+            out=scale_cols[:].rearrange("p (g t) -> p g t", t=PACK),
+            in_=Wq_scale.rearrange("o (g p t) -> p (o g) t", p=P, t=PACK),
+        )
+
+        wq_bytes_sb = {}
+        hs_sb = {}
+
+        def load_scale(c):
+            cols = slice(c * CHUNK, (c + 1) * CHUNK)
+            nc.sync.dma_start(out=scale_all[:, cols], in_=scale_row[cols].partition_broadcast(P))
+
+        def load_w(i):
+            wq_bytes_sb[i] = keep.tile([P, E], U8, name="wq_bytes_sb%d" % i)
+            nc.sync.dma_start(out=wq_bytes_sb[i][:], in_=Wq_bytes[i * P:(i + 1) * P, :])
+
+        def load_h(m):
+            hs_sb[m] = keep.tile([P, E], BF16, name="hs_sb%d" % m)
+            nc.sync.dma_start(out=hs_sb[m][:], in_=hidden_states[m * P:(m + 1) * P, :])
+
+        load_scale(0)
+        load_w(0)
+        for c in range(1, E // CHUNK):
+            load_scale(c)
+        load_w(1)
+        load_w(SCALAR_TILES[0])
+        load_h(0)
+        load_h(1)
+        load_w(2)
+        load_h(2)
+        load_h(3)
+        for i in range(3, H):
+            if i != SCALAR_TILES[0]:
+                load_w(i)
+
+        gain = const.tile([P, TOKEN_TILES * D], F32, name="gain")
+        for m in range(TOKEN_TILES):
+            nc.scalar.copy(out=gain[:, m * D:(m + 1) * D], in_=gain_bf[:])
+        squares_unused = const.tile([P, D], F32, name="squares_unused")
+
+        wide = {}
+        banks = {}
+        planes = {}
+        grouped = {}
+        codes = {}
+        scales = {}
+        acc = {}
+        rstd = {}
+
+        def widen_on_vector(i, cols):
+            if i not in wide:
+                wide[i] = wide_pool.tile([P, E], BF16, name="wide")
+            nc.vector.tensor_tensor(
+                out=wide[i][:, cols],
+                in0=wq_bytes_sb[i][:, cols].bitcast(FP8),
+                in1=scale_all[:, cols],
+                op=MULT,
+            )
+
+        def cast_on_scalar(i):
+            wide[i] = wide_pool.tile([P, E], BF16, name="wide")
+            nc.scalar.copy(out=wide[i][:], in_=wq_bytes_sb[i][:].bitcast(FP8))
+
+        def turn(unit):
+            kind, idx = unit
+            src = wide[idx] if kind == "w" else hs_sb[idx]
+            words = src[:].bitcast(F32)
+            banks[unit] = []
+            for b in range(2):
+                xt = turn_psum.tile([P, 2, 2 * P], F32, name="xt")
+                for g2 in range(2):
+                    g = 2 * b + g2
+                    for u in range(2):
+                        nc.tensor.transpose(
+                            xt[:, u, g2 * P:(g2 + 1) * P],
+                            words[:, 256 * g + u:256 * (g + 1):2],
+                            ident[:],
+                        )
+                banks[unit].append(xt)
+
+        def copy_out(unit):
+            grouped[unit] = grouped_pool.tile([P, E], BF16, name="grouped", align_bytes=64)
+            grouped_words = grouped[unit][:].bitcast(F32)
+            for b in range(2):
+                nc.scalar.copy(
+                    out=grouped_words[:, b * 512:(b + 1) * 512].rearrange("p (r u) -> p r u", u=2),
+                    in_=banks[unit][b][:].rearrange("p u r -> p r u"),
+                )
+
+        def scale_out_of_psum(i):
+            planes[i] = plane_pool.tile([P, E], BF16, name="planes")
+            for b in range(2):
+                halves = banks[("w", i)][b][:].bitcast(BF16).rearrange("p u (g r e) -> p u g r e", g=2, e=2)
+                for g2 in range(2):
+                    for u in range(2):
+                        for e in range(2):
+                            col = (2 * b + g2) * PACK + 2 * u + e
+                            nc.scalar.activation(
+                                out=planes[i][:, col * P:(col + 1) * P], in_=halves[:, u, g2, :, e],
+                                func=ACT.Copy, scale=scale_cols[:, col:col + 1],
+                            )
+
+        def interleave_on_scalar(i):
+            unit = ("w", i)
+            grouped[unit] = grouped_pool.tile([P, E], BF16, name="grouped", align_bytes=64)
+            nc.scalar.copy(
+                out=grouped[unit][:].rearrange("p (g r t) -> p g r t", g=PASSES, t=PACK),
+                in_=planes[i][:].rearrange("p (g t r) -> p g r t", g=PASSES, t=PACK),
+            )
+
+        def quantize(unit):
+            codes[unit] = keep.tile([P, PASSES * P], U32, name="codes_%s%d" % unit, align_bytes=64)
+            scales[unit] = keep.tile([P, PASSES * P], U8, name="scales_%s%d" % unit, align_bytes=64)
+            nc.vector.quantize_mx(
+                out=codes[unit][:].bitcast(FP8X4),
+                scales=scales[unit][:],
+                in_=grouped[unit][:],
+            )
+
+        def multiply(i):
+            acc[i] = acc_psum.tile([P, TOKEN_TILES * D], F32, name="acc")
+            for m in range(TOKEN_TILES):
+                for g in range(PASSES):
+                    cols = slice(g * P, (g + 1) * P)
+                    nc.tensor.matmul_mx(
+                        out=acc[i][:, m * D:(m + 1) * D],
+                        lhsT=codes[("h", m)][:, cols].bitcast(FP8X4),
+                        lhsT_scale=scales[("h", m)][:, cols],
+                        rhs=codes[("w", i)][:, cols].bitcast(FP8X4),
+                        rhs_scale=scales[("w", i)][:, cols],
+                        start=(g == 0),
+                        stop=(g == PASSES - 1),
+                    )
+
+        def inverse_rms(i):
+            sumsq = stat_pool.tile([P, TOKEN_TILES], F32, name="sumsq")
+            for m in range(TOKEN_TILES):
+                nc.scalar.activation(
+                    out=squares_unused[:], in_=acc[i][:, m * D:(m + 1) * D], func=ACT.Square,
+                    accum_out=sumsq[:, m:m + 1],
+                )
+            rstd[i] = stat_pool.tile([P, TOKEN_TILES], F32, name="rstd")
+            nc.scalar.activation(out=rstd[i][:], in_=sumsq[:], func=ACT.Abs_reciprocal_sqrt, scale=1.0 / D, bias=EPS)
+
+        def finish(i):
+            res = result_pool.tile([P, TOKEN_TILES * D], F32, name="res")
+            for m in range(TOKEN_TILES):
+                nc.vector.scalar_tensor_tensor(
+                    out=res[:, m * D:(m + 1) * D], in0=acc[i][:, m * D:(m + 1) * D],
+                    scalar=rstd[i][:, m:m + 1], in1=gain[:, m * D:(m + 1) * D],
+                    op0=MULT, op1=MULT,
+                )
+            nc.sync.dma_start(
+                out=out[i].rearrange("(m p) d -> p m d", p=P),
+                in_=res[:].rearrange("p (m d) -> p m d", m=TOKEN_TILES),
+            )
+
+        def is_tile(i):
+            return 0 <= i < H
+
+        def on_vectors_road(i):
+            return is_tile(i) and i not in SCALAR_TILES
+
+        for j in range(H + FINISH_LAG + 1):
+            if j == 0:
+                for c in range(E // CHUNK):
+                    widen_on_vector(0, slice(c * CHUNK, (c + 1) * CHUNK))
+            elif on_vectors_road(j):
+                widen_on_vector(j, slice(0, E))
+
+            if on_vectors_road(j - TURN_LAG):
+                turn(("w", j - TURN_LAG))
+            for m in TOKENS_TURNED.get(j, ()):
+                turn(("h", m))
+            if is_tile(j - MULTIPLY_LAG):
+                multiply(j - MULTIPLY_LAG)
+            if j + SCALE_LEAD in SCALAR_TILES:
+                turn(("w", j + SCALE_LEAD))
+
+            if on_vectors_road(j - TURN_LAG):
+                copy_out(("w", j - TURN_LAG))
+            for m in TOKENS_TURNED.get(j, ()):
+                copy_out(("h", m))
+            if is_tile(j - MULTIPLY_LAG):
+                inverse_rms(j - MULTIPLY_LAG)
+            if j + INTERLEAVE_LEAD in SCALAR_TILES:
+                interleave_on_scalar(j + INTERLEAVE_LEAD)
+            if j + SCALE_LEAD in SCALAR_TILES:
+                scale_out_of_psum(j + SCALE_LEAD)
+            if j + CAST_LEAD in SCALAR_TILES:
+                cast_on_scalar(j + CAST_LEAD)
+
+            if is_tile(j - QUANTIZE_LAG):
+                quantize(("w", j - QUANTIZE_LAG))
+            for m in TOKENS_QUANTIZED.get(j, ()):
+                quantize(("h", m))
+            if is_tile(j - FINISH_LAG):
+                finish(j - FINISH_LAG)

@@ -56,24 +56,19 @@ def tile_combcrossattention_pa_kernel(tc, hidden_states, Wq_bytes, Wq_scale, q_n
         warm = const.tile([P, 1], F32, name="warm")
         nc.scalar.activation(out=warm[:], in_=one[:], func=ACT.Abs_reciprocal_sqrt)
 
-        scale_row = Wq_scale.rearrange("o k -> (o k)")
         scale_all = const.tile([P, E], F32, name="scale_all")
 
         gain_bf = const.tile([P, D], BF16, name="gain_bf")
         nc.scalar.dma_start(out=gain_bf[:], in_=q_norm_w.partition_broadcast(P))
 
         scale_cols = const.tile([P, PACK * PASSES], F32, name="scale_cols")
-        nc.scalar.dma_start(
+        nc.sync.dma_start(
             out=scale_cols[:].rearrange("p (g t) -> p g t", t=PACK),
             in_=Wq_scale.rearrange("o (g p t) -> p (o g) t", p=P, t=PACK),
         )
 
         wq_bytes_sb = {}
         hs_sb = {}
-
-        def load_scale(c):
-            cols = slice(c * CHUNK, (c + 1) * CHUNK)
-            nc.sync.dma_start(out=scale_all[:, cols], in_=scale_row[cols].partition_broadcast(P))
 
         def load_w(i):
             wq_bytes_sb[i] = keep.tile([P, E], U8, name="wq_bytes_sb%d" % i)
@@ -83,10 +78,7 @@ def tile_combcrossattention_pa_kernel(tc, hidden_states, Wq_bytes, Wq_scale, q_n
             hs_sb[m] = keep.tile([P, E], BF16, name="hs_sb%d" % m)
             nc.sync.dma_start(out=hs_sb[m][:], in_=hidden_states[m * P:(m + 1) * P, :])
 
-        load_scale(0)
         load_w(0)
-        for c in range(1, E // CHUNK):
-            load_scale(c)
         load_w(1)
         load_w(SCALAR_TILES[0])
         load_h(0)
@@ -97,6 +89,18 @@ def tile_combcrossattention_pa_kernel(tc, hidden_states, Wq_bytes, Wq_scale, q_n
         for i in range(3, H):
             if i != SCALAR_TILES[0]:
                 load_w(i)
+
+        for g in range(PASSES):
+            spread = turn_psum.tile([P, 2, 2 * P], F32, name="xt")
+            spread_t = spread[:].rearrange("p u (h n) -> p (u h) n", h=2)
+            for t in range(PACK):
+                col = g * PACK + t
+                nc.tensor.transpose(spread_t[:, t, :], scale_cols[:, col:col + 1].to_broadcast([P, P]), ident[:])
+            dst = scale_all[:, g * CHUNK:(g + 1) * CHUNK].rearrange("p (n t) -> p n t", t=PACK)
+            if g == 0:
+                nc.vector.tensor_copy(out=dst, in_=spread_t.rearrange("p t n -> p n t"))
+            else:
+                nc.scalar.copy(out=dst, in_=spread_t.rearrange("p t n -> p n t"))
 
         gain = const.tile([P, TOKEN_TILES * D], F32, name="gain")
         for m in range(TOKEN_TILES):

@@ -25,14 +25,18 @@ CHUNK = 512
 SCALAR_TILES = (4, 10)
 
 TURN_LAG = 1
-QUANTIZE_LAG = 2
-MULTIPLY_LAG = 4
-FINISH_LAG = 5
+COPY_LAG = 2
+QUANTIZE_LAG = 3
+MULTIPLY_LAG = 5
+SQUARE_LAG = 6
+FINISH_LAG = 7
 CAST_LEAD = 3
-SCALE_LEAD = 2
-INTERLEAVE_LEAD = 1
+TURN_LEAD = 2
+SCALE_LEAD = 1
+INTERLEAVE_LEAD = 0
 TOKENS_TURNED = {1: (0, 1), 2: (2, 3)}
-TOKENS_QUANTIZED = {2: (0, 1), 3: (2, 3)}
+TOKENS_COPIED = {2: (0, 1), 3: (2, 3)}
+TOKENS_QUANTIZED = {3: (0, 1), 4: (2, 3)}
 
 
 def tile_combcrossattention_pa_kernel(tc, hidden_states, Wq_bytes, Wq_scale, q_norm_w, out):
@@ -243,15 +247,15 @@ def tile_combcrossattention_pa_kernel(tc, hidden_states, Wq_bytes, Wq_scale, q_n
                 turn(("h", m))
             if is_tile(j - MULTIPLY_LAG):
                 multiply(j - MULTIPLY_LAG)
-            if j + SCALE_LEAD in SCALAR_TILES:
-                turn(("w", j + SCALE_LEAD))
+            if j + TURN_LEAD in SCALAR_TILES:
+                turn(("w", j + TURN_LEAD))
 
-            if on_vectors_road(j - TURN_LAG):
-                copy_out(("w", j - TURN_LAG))
-            for m in TOKENS_TURNED.get(j, ()):
+            if on_vectors_road(j - COPY_LAG):
+                copy_out(("w", j - COPY_LAG))
+            for m in TOKENS_COPIED.get(j, ()):
                 copy_out(("h", m))
-            if is_tile(j - MULTIPLY_LAG):
-                inverse_rms(j - MULTIPLY_LAG)
+            if is_tile(j - SQUARE_LAG):
+                inverse_rms(j - SQUARE_LAG)
             if j + INTERLEAVE_LEAD in SCALAR_TILES:
                 interleave_on_scalar(j + INTERLEAVE_LEAD)
             if j + SCALE_LEAD in SCALAR_TILES:

@@ -63,7 +63,6 @@ def tile_combcrossattention_pa_kernel(tc, hidden_states, Wq_bytes, Wq_scale, q_n
         scale_all = const.tile([P, E], F32, name="scale_all")
 
         gain_bf = const.tile([P, D], BF16, name="gain_bf")
-        nc.scalar.dma_start(out=gain_bf[:], in_=q_norm_w.partition_broadcast(P))
 
         scale_cols = const.tile([P, PACK * PASSES], F32, name="scale_cols")
         nc.sync.dma_start(
@@ -80,19 +79,20 @@ def tile_combcrossattention_pa_kernel(tc, hidden_states, Wq_bytes, Wq_scale, q_n
 
         def load_h(m):
             hs_sb[m] = keep.tile([P, E], BF16, name="hs_sb%d" % m)
-            nc.sync.dma_start(out=hs_sb[m][:], in_=hidden_states[m * P:(m + 1) * P, :])
+            nc.sync.dma_start(out=hs_sb[m][:], in_=hidden_states.rearrange("(p m) k -> m p k", m=TOKEN_TILES)[m])
 
         load_w(0)
         load_w(1)
+        nc.sync.dma_start(out=gain_bf[:], in_=q_norm_w.partition_broadcast(P))
+        load_w(2)
         load_w(SCALAR_TILES[0])
         load_h(0)
+        load_w(3)
         load_h(1)
-        load_w(2)
         load_h(2)
         load_h(3)
-        for i in range(3, H):
-            if i != SCALAR_TILES[0]:
-                load_w(i)
+        for i in range(5, H):
+            load_w(i)
 
         for g in range(PASSES):
             spread = turn_psum.tile([P, 2, 2 * P], F32, name="xt")
@@ -106,9 +106,8 @@ def tile_combcrossattention_pa_kernel(tc, hidden_states, Wq_bytes, Wq_scale, q_n
             else:
                 nc.scalar.copy(out=dst, in_=spread_t.rearrange("p t n -> p n t"))
 
-        gain = const.tile([P, TOKEN_TILES * D], F32, name="gain")
-        for m in range(TOKEN_TILES):
-            nc.scalar.copy(out=gain[:, m * D:(m + 1) * D], in_=gain_bf[:])
+        gain = const.tile([P, D], F32, name="gain")
+        nc.scalar.copy(out=gain[:], in_=gain_bf[:])
         squares_unused = const.tile([P, D], F32, name="squares_unused")
 
         wide = {}
@@ -220,13 +219,16 @@ def tile_combcrossattention_pa_kernel(tc, hidden_states, Wq_bytes, Wq_scale, q_n
             for m in range(TOKEN_TILES):
                 nc.vector.scalar_tensor_tensor(
                     out=res[:, m * D:(m + 1) * D], in0=acc[i][:, m * D:(m + 1) * D],
-                    scalar=rstd[i][:, m:m + 1], in1=gain[:, m * D:(m + 1) * D],
+                    scalar=rstd[i][:, m:m + 1], in1=gain[:],
                     op0=MULT, op1=MULT,
                 )
-            nc.sync.dma_start(
-                out=out[i].rearrange("(m p) d -> p m d", p=P),
-                in_=res[:].rearrange("p (m d) -> p m d", m=TOKEN_TILES),
-            )
+                if i == H - 1:
+                    nc.sync.dma_start(
+                        out=out[i].rearrange("(p m) d -> p m d", m=TOKEN_TILES)[:, m, :],
+                        in_=res[:, m * D:(m + 1) * D],
+                    )
+            if i < H - 1:
+                nc.sync.dma_start(out=out[i].rearrange("(p m) d -> p (m d)", m=TOKEN_TILES), in_=res[:])
 
         def is_tile(i):
             return 0 <= i < H

@@ -124,8 +124,8 @@ def tile_combcrossattention_pa_kernel(tc, hidden_states, Wq_bytes, Wq_scale, q_n
                 wide[i] = wide_pool.tile([P, E], BF16, name="wide")
             nc.vector.tensor_tensor(
                 out=wide[i][:, cols],
-                in0=wq_bytes_sb[i][:, cols].bitcast(FP8),
-                in1=scale_all[:, cols],
+                in0=scale_all[:, cols],
+                in1=wq_bytes_sb[i][:, cols].bitcast(FP8),
                 op=MULT,
             )
 

@@ -48,7 +48,7 @@ def tile_combcrossattention_pa_kernel(tc, hidden_states, Wq_bytes, Wq_scale, q_n
         grouped_pool = ctx.enter_context(tc.tile_pool(name="grouped", bufs=5))
         plane_pool = ctx.enter_context(tc.tile_pool(name="planes", bufs=2))
         stat_pool = ctx.enter_context(tc.tile_pool(name="stat", bufs=6))
-        result_pool = ctx.enter_context(tc.tile_pool(name="result", bufs=4))
+        result_pool = ctx.enter_context(tc.tile_pool(name="result", bufs=8))
         turn_psum = ctx.enter_context(tc.psum_pool(name="turn_psum", bufs=4))
         acc_psum = ctx.enter_context(tc.psum_pool(name="acc_psum", bufs=4))
 
@@ -83,7 +83,6 @@ def tile_combcrossattention_pa_kernel(tc, hidden_states, Wq_bytes, Wq_scale, q_n
 
         load_w(0)
         load_w(1)
-        nc.sync.dma_start(out=gain_bf[:], in_=q_norm_w.partition_broadcast(P))
         load_w(2)
         load_w(SCALAR_TILES[0])
         load_h(0)
@@ -93,6 +92,7 @@ def tile_combcrossattention_pa_kernel(tc, hidden_states, Wq_bytes, Wq_scale, q_n
         load_h(3)
         for i in range(5, H):
             load_w(i)
+        nc.sync.dma_start(out=gain_bf[:], in_=q_norm_w.partition_broadcast(P))
 
         for g in range(PASSES):
             spread = turn_psum.tile([P, 2, 2 * P], F32, name="xt")
@@ -106,8 +106,6 @@ def tile_combcrossattention_pa_kernel(tc, hidden_states, Wq_bytes, Wq_scale, q_n
             else:
                 nc.scalar.copy(out=dst, in_=spread_t.rearrange("p t n -> p n t"))
 
-        gain = const.tile([P, D], F32, name="gain")
-        nc.scalar.copy(out=gain[:], in_=gain_bf[:])
         squares_unused = const.tile([P, D], F32, name="squares_unused")
 
         wide = {}
@@ -219,7 +217,7 @@ def tile_combcrossattention_pa_kernel(tc, hidden_states, Wq_bytes, Wq_scale, q_n
             for m in range(TOKEN_TILES):
                 nc.vector.scalar_tensor_tensor(
                     out=res[:, m * D:(m + 1) * D], in0=acc[i][:, m * D:(m + 1) * D],
-                    scalar=rstd[i][:, m:m + 1], in1=gain[:],
+                    scalar=rstd[i][:, m:m + 1], in1=gain_bf[:],
                     op0=MULT, op1=MULT,
                 )
                 if i == H - 1:

from contextlib import ExitStack

import concourse.mybir as mybir
from concourse.masks import make_identity

T, E, H, D = 512, 2048, 16, 128
EPS = 1e-05
FLOPS = 2 * T * E * H * D

F32 = mybir.dt.float32
BF16 = mybir.dt.bfloat16
U32 = mybir.dt.uint32
U8 = mybir.dt.uint8
FP8 = mybir.dt.float8_e4m3fn
FP8X4 = mybir.dt.float8_e4m3fn_x4
ACT = mybir.ActivationFunctionType
MULT = mybir.AluOpType.mult

P = 128
PACK = 4
PASSES = E // (P * PACK)
TOKEN_TILES = T // P
CHUNK = 512

SCALAR_TILES = (4, 10)

TURN_LAG = 1
COPY_LAG = 2
QUANTIZE_LAG = 3
MULTIPLY_LAG = 5
SQUARE_LAG = 6
FINISH_LAG = 7
CAST_LEAD = 3
TURN_LEAD = 2
SCALE_LEAD = 1
INTERLEAVE_LEAD = 0
TOKENS_TURNED = {1: (0, 1), 2: (2, 3)}
TOKENS_COPIED = {2: (0, 1), 3: (2, 3)}
TOKENS_QUANTIZED = {3: (0, 1), 4: (2, 3)}


def tile_combcrossattention_pa_kernel(tc, hidden_states, Wq_bytes, Wq_scale, q_norm_w, out):
    nc = tc.nc
    with ExitStack() as ctx:
        const = ctx.enter_context(tc.tile_pool(name="const", bufs=1))
        keep = ctx.enter_context(tc.tile_pool(name="keep", bufs=1))
        wide_pool = ctx.enter_context(tc.tile_pool(name="wide", bufs=5))
        grouped_pool = ctx.enter_context(tc.tile_pool(name="grouped", bufs=5))
        plane_pool = ctx.enter_context(tc.tile_pool(name="planes", bufs=2))
        stat_pool = ctx.enter_context(tc.tile_pool(name="stat", bufs=6))
        result_pool = ctx.enter_context(tc.tile_pool(name="result", bufs=8))
        turn_psum = ctx.enter_context(tc.psum_pool(name="turn_psum", bufs=4))
        acc_psum = ctx.enter_context(tc.psum_pool(name="acc_psum", bufs=4))

        ident = const.tile([P, P], F32, name="ident")
        make_identity(nc, ident[:])

        one = const.tile([P, 1], F32, name="one")
        nc.gpsimd.memset(one[:], 1.0)
        warm = const.tile([P, 1], F32, name="warm")
        nc.scalar.activation(out=warm[:], in_=one[:], func=ACT.Abs_reciprocal_sqrt)

        scale_all = const.tile([P, E], F32, name="scale_all")

        gain_bf = const.tile([P, D], BF16, name="gain_bf")

        scale_cols = const.tile([P, PACK * PASSES], F32, name="scale_cols")
        nc.sync.dma_start(
            out=scale_cols[:].rearrange("p (g t) -> p g t", t=PACK),
            in_=Wq_scale.rearrange("o (g p t) -> p (o g) t", p=P, t=PACK),
        )

        wq_bytes_sb = {}
        hs_sb = {}

        def load_w(i):
            wq_bytes_sb[i] = keep.tile([P, E], U8, name="wq_bytes_sb%d" % i)
            nc.sync.dma_start(out=wq_bytes_sb[i][:], in_=Wq_bytes[i * P:(i + 1) * P, :])

        def load_h(m):
            hs_sb[m] = keep.tile([P, E], BF16, name="hs_sb%d" % m)
            nc.sync.dma_start(out=hs_sb[m][:], in_=hidden_states.rearrange("(p m) k -> m p k", m=TOKEN_TILES)[m])

        load_w(0)
        load_w(1)
        load_w(2)
        load_w(SCALAR_TILES[0])
        load_h(0)
        load_w(3)
        load_h(1)
        load_h(2)
        load_h(3)
        for i in range(5, H):
            load_w(i)
        nc.sync.dma_start(out=gain_bf[:], in_=q_norm_w.partition_broadcast(P))

        for g in range(PASSES):
            spread = turn_psum.tile([P, 2, 2 * P], F32, name="xt")
            spread_t = spread[:].rearrange("p u (h n) -> p (u h) n", h=2)
            for t in range(PACK):
                col = g * PACK + t
                nc.tensor.transpose(spread_t[:, t, :], scale_cols[:, col:col + 1].to_broadcast([P, P]), ident[:])
            dst = scale_all[:, g * CHUNK:(g + 1) * CHUNK].rearrange("p (n t) -> p n t", t=PACK)
            if g == 0:
                nc.vector.tensor_copy(out=dst, in_=spread_t.rearrange("p t n -> p n t"))
            else:
                nc.scalar.copy(out=dst, in_=spread_t.rearrange("p t n -> p n t"))

        squares_unused = const.tile([P, D], F32, name="squares_unused")

        wide = {}
        banks = {}
        planes = {}
        grouped = {}
        codes = {}
        scales = {}
        acc = {}
        rstd = {}

        def widen_on_vector(i, cols):
            if i not in wide:
                wide[i] = wide_pool.tile([P, E], BF16, name="wide")
            nc.vector.tensor_tensor(
                out=wide[i][:, cols],
                in0=scale_all[:, cols],
                in1=wq_bytes_sb[i][:, cols].bitcast(FP8),
                op=MULT,
            )

        def cast_on_scalar(i):
            wide[i] = wide_pool.tile([P, E], BF16, name="wide")
            nc.scalar.copy(out=wide[i][:], in_=wq_bytes_sb[i][:].bitcast(FP8))

        def turn(unit):
            kind, idx = unit
            src = wide[idx] if kind == "w" else hs_sb[idx]
            words = src[:].bitcast(F32)
            banks[unit] = []
            for b in range(2):
                xt = turn_psum.tile([P, 2, 2 * P], F32, name="xt")
                for g2 in range(2):
                    g = 2 * b + g2
                    for u in range(2):
                        nc.tensor.transpose(
                            xt[:, u, g2 * P:(g2 + 1) * P],
                            words[:, 256 * g + u:256 * (g + 1):2],
                            ident[:],
                        )
                banks[unit].append(xt)

        def copy_out(unit):
            grouped[unit] = grouped_pool.tile([P, E], BF16, name="grouped", align_bytes=64)
            grouped_words = grouped[unit][:].bitcast(F32)
            for b in range(2):
                nc.scalar.copy(
                    out=grouped_words[:, b * 512:(b + 1) * 512].rearrange("p (r u) -> p r u", u=2),
                    in_=banks[unit][b][:].rearrange("p u r -> p r u"),
                )

        def scale_out_of_psum(i):
            planes[i] = plane_pool.tile([P, E], BF16, name="planes")
            for b in range(2):
                halves = banks[("w", i)][b][:].bitcast(BF16).rearrange("p u (g r e) -> p u g r e", g=2, e=2)
                for g2 in range(2):
                    for u in range(2):
                        for e in range(2):
                            col = (2 * b + g2) * PACK + 2 * u + e
                            nc.scalar.activation(
                                out=planes[i][:, col * P:(col + 1) * P], in_=halves[:, u, g2, :, e],
                                func=ACT.Copy, scale=scale_cols[:, col:col + 1],
                            )

        def interleave_on_scalar(i):
            unit = ("w", i)
            grouped[unit] = grouped_pool.tile([P, E], BF16, name="grouped", align_bytes=64)
            nc.scalar.copy(
                out=grouped[unit][:].rearrange("p (g r t) -> p g r t", g=PASSES, t=PACK),
                in_=planes[i][:].rearrange("p (g t r) -> p g r t", g=PASSES, t=PACK),
            )

        def quantize(unit):
            codes[unit] = keep.tile([P, PASSES * P], U32, name="codes_%s%d" % unit, align_bytes=64)
            scales[unit] = keep.tile([P, PASSES * P], U8, name="scales_%s%d" % unit, align_bytes=64)
            nc.vector.quantize_mx(
                out=codes[unit][:].bitcast(FP8X4),
                scales=scales[unit][:],
                in_=grouped[unit][:],
            )

        def multiply(i):
            acc[i] = acc_psum.tile([P, TOKEN_TILES * D], F32, name="acc")
            for m in range(TOKEN_TILES):
                for g in range(PASSES):
                    cols = slice(g * P, (g + 1) * P)
                    nc.tensor.matmul_mx(
                        out=acc[i][:, m * D:(m + 1) * D],
                        lhsT=codes[("h", m)][:, cols].bitcast(FP8X4),
                        lhsT_scale=scales[("h", m)][:, cols],
                        rhs=codes[("w", i)][:, cols].bitcast(FP8X4),
                        rhs_scale=scales[("w", i)][:, cols],
                        start=(g == 0),
                        stop=(g == PASSES - 1),
                    )

        def inverse_rms(i):
            sumsq = stat_pool.tile([P, TOKEN_TILES], F32, name="sumsq")
            for m in range(TOKEN_TILES):
                nc.scalar.activation(
                    out=squares_unused[:], in_=acc[i][:, m * D:(m + 1) * D], func=ACT.Square,
                    accum_out=sumsq[:, m:m + 1],
                )
            rstd[i] = stat_pool.tile([P, TOKEN_TILES], F32, name="rstd")
            nc.scalar.activation(out=rstd[i][:], in_=sumsq[:], func=ACT.Abs_reciprocal_sqrt, scale=1.0 / D, bias=EPS)

        def finish(i):
            res = result_pool.tile([P, TOKEN_TILES * D], F32, name="res")
            for m in range(TOKEN_TILES):
                nc.vector.scalar_tensor_tensor(
                    out=res[:, m * D:(m + 1) * D], in0=acc[i][:, m * D:(m + 1) * D],
                    scalar=rstd[i][:, m:m + 1], in1=gain_bf[:],
                    op0=MULT, op1=MULT,
                )
                if i == H - 1:
                    nc.sync.dma_start(
                        out=out[i].rearrange("(p m) d -> p m d", m=TOKEN_TILES)[:, m, :],
                        in_=res[:, m * D:(m + 1) * D],
                    )
            if i < H - 1:
                nc.sync.dma_start(out=out[i].rearrange("(p m) d -> p (m d)", m=TOKEN_TILES), in_=res[:])

        def is_tile(i):
            return 0 <= i < H

        def on_vectors_road(i):
            return is_tile(i) and i not in SCALAR_TILES

        for j in range(H + FINISH_LAG + 1):
            if j == 0:
                for c in range(E // CHUNK):
                    widen_on_vector(0, slice(c * CHUNK, (c + 1) * CHUNK))
            elif on_vectors_road(j):
                widen_on_vector(j, slice(0, E))

            if on_vectors_road(j - TURN_LAG):
                turn(("w", j - TURN_LAG))
            for m in TOKENS_TURNED.get(j, ()):
                turn(("h", m))
            if is_tile(j - MULTIPLY_LAG):
                multiply(j - MULTIPLY_LAG)
            if j + TURN_LEAD in SCALAR_TILES:
                turn(("w", j + TURN_LEAD))

            if on_vectors_road(j - COPY_LAG):
                copy_out(("w", j - COPY_LAG))
            for m in TOKENS_COPIED.get(j, ()):
                copy_out(("h", m))
            if is_tile(j - SQUARE_LAG):
                inverse_rms(j - SQUARE_LAG)
            if j + INTERLEAVE_LEAD in SCALAR_TILES:
                interleave_on_scalar(j + INTERLEAVE_LEAD)
            if j + SCALE_LEAD in SCALAR_TILES:
                scale_out_of_psum(j + SCALE_LEAD)
            if j + CAST_LEAD in SCALAR_TILES:
                cast_on_scalar(j + CAST_LEAD)

            if is_tile(j - QUANTIZE_LAG):
                quantize(("w", j - QUANTIZE_LAG))
            for m in TOKENS_QUANTIZED.get(j, ()):
                quantize(("h", m))
            if is_tile(j - FINISH_LAG):
                finish(j - FINISH_LAG)
